import numpy as np
import ml_dtypes


def mxq(x, axis, fmt="e4m3"):
    dtype, down = {"e4m3": (ml_dtypes.float8_e4m3fn, 7), "e5m2": (ml_dtypes.float8_e5m2, 14)}[fmt]
    v = np.moveaxis(np.asarray(x, np.float32).astype(ml_dtypes.bfloat16).astype(np.float64), axis, -1)
    blocks = v.reshape(v.shape[:-1] + (-1, 32))
    amax = np.abs(blocks).max(-1, keepdims=True)
    byte = np.maximum(np.where(amax > 0, np.frexp(amax)[1] - 1 + 127, 0) - down, 1)
    scale = np.exp2(byte - 127.0)
    codes = (blocks / scale).astype(np.float32).astype(dtype).astype(np.float64)
    return np.moveaxis((codes * scale).reshape(v.shape), -1, axis)


WIDE = False


def mx_kscale(k):
    if not WIDE:
        return np.ones(k)
    levels = np.array([10, -10, 5, -5, 0])
    a = np.random.permutation(np.resize(levels, k // 512 * 4)).reshape(k // 512, 4)
    idx = np.arange(k)
    return np.exp2(a[idx // 512, idx % 128 // 32])


BF16 = ml_dtypes.bfloat16


def bf(x):
    return np.asarray(x, np.float32).astype(BF16)


def f64(x):
    return np.asarray(x).astype(np.float64)


E2M1 = np.array([0.0, 0.5, 1.0, 1.5, 2.0, 3.0, 4.0, 6.0, -0.0, -0.5, -1.0, -1.5, -2.0, -3.0, -4.0, -6.0])


def pack_weight(w, fmt):
    k, n = w.shape
    w = f64(bf(w)).reshape(k // 32, 32, n)
    amax = np.abs(w).max(1)
    if fmt == "e4m3":
        byte = np.frexp(amax)[1] - 1 + 127 - 7
    else:
        mant, ex = np.frexp(amax / 6.0)
        byte = np.where(mant > 0.5, ex, ex - 1) + 127
    byte = np.clip(np.where(amax > 0, byte, 1), 1, 254)
    scaled = (w * np.exp2(127.0 - byte)[:, None, :]).reshape(k, n).astype(np.float32)
    by_word = np.ascontiguousarray(scaled.reshape(k // 512, 128, 4, n).transpose(0, 1, 3, 2))
    if fmt == "e4m3":
        words = by_word.astype(ml_dtypes.float8_e4m3fn).view(np.uint8)
    else:
        c = by_word.astype(ml_dtypes.float4_e2m1fn).view(np.uint8) & 0xF
        words = c[..., 0::2] | (c[..., 1::2] << 4)
    return np.ascontiguousarray(words), np.ascontiguousarray(byte.astype(np.uint8).reshape(k // 512, 16, n))


def unpack_weight(words, scales, fmt):
    g, p, n, _ = words.shape
    if fmt == "e4m3":
        vals = np.ascontiguousarray(words).view(ml_dtypes.float8_e4m3fn).astype(np.float64)
    else:
        nib = np.empty((g, p, n, 4), np.uint8)
        nib[..., 0::2] = words & 0xF
        nib[..., 1::2] = words >> 4
        vals = E2M1[nib]
    vals = vals * np.repeat(np.exp2(scales.astype(np.float64) - 127.0), 8, axis=1)[..., None]
    return vals.transpose(0, 1, 3, 2).reshape(g * 512, n)


S, B, SC = 128, 6144, 4096


def setup_inputs():
    s = mx_kscale(B)
    proba = bf((np.random.standard_normal((S, B)) * s).reshape(-1))
    cur_inven = bf(np.random.random_sample((S, SC)))
    words, scales = pack_weight(np.random.random_sample((B, SC)) * (16.0 / np.sqrt(B)) / s[:, None], "e4m3")
    avail_bundle = bf(np.random.random_sample(B) * s)
    alloc_bundle = bf(np.random.random_sample(B) * s)
    return {"proba": proba,
            "cur_inven": cur_inven,
            "bun_sc_words": words,
            "bun_sc_scales": scales,
            "avail_bundle": avail_bundle,
            "alloc_bundle": alloc_bundle}


def reference(proba, cur_inven, bun_sc_words, bun_sc_scales, avail_bundle, alloc_bundle):
    p = f64(proba).reshape(S, B)
    av = f64(avail_bundle)
    al = f64(alloc_bundle)
    over_avail = (av[None, :] - p < 0.0) & (p > 0.0)
    over_alloc = (al[None, :] + p < 0.0) & (p < 0.0)
    cm = np.where(over_avail | over_alloc, 0.01, 1.0)
    next_inven = f64(cur_inven) + (mxq(p * cm, 1, "e4m3") @ unpack_weight(bun_sc_words, bun_sc_scales, "e4m3"))
    return next_inven.reshape(1, -1)

@@ -1,0 +1,206 @@
+from contextlib import ExitStack
+
+import concourse.mybir as mybir
+from concourse.masks import make_identity
+
+BF16 = mybir.dt.bfloat16
+F32 = mybir.dt.float32
+I32 = mybir.dt.int32
+U32 = mybir.dt.uint32
+U8 = mybir.dt.uint8
+FP8X4 = mybir.dt.float8_e4m3fn_x4
+ALU = mybir.AluOpType
+
+P = 128
+S = 128
+B = 6144
+SC = 4096
+PACK = 4
+K_PASS = P * PACK
+G = B // K_PASS
+N_TILE = 512
+NB = SC // N_TILE
+G_CHUNK = 2
+CHUNKS = G // G_CHUNK
+CHUNK_COLS = G_CHUNK * S * PACK
+W_BUFS = 7
+PLANES_PER_TILE = 4
+
+FLOPS = 2 * S * B * SC
+
+
+def tile_optblockv2_w_kernel(
+    tc, proba, cur_inven, bun_sc_words, bun_sc_scales, avail_bundle, alloc_bundle, out
+):
+    nc = tc.nc
+    x_dram = proba.rearrange("(s b) -> s b", b=B)
+    out_rows = out.rearrange("o (s n) -> (o s) n", n=SC)
+
+    with ExitStack() as ctx:
+        const = ctx.enter_context(tc.tile_pool(name="const", bufs=1))
+        wpool = ctx.enter_context(tc.tile_pool(name="wpool", bufs=W_BUFS))
+        work = ctx.enter_context(tc.tile_pool(name="work", bufs=2))
+        opool = ctx.enter_context(tc.tile_pool(name="opool", bufs=NB))
+        psum = ctx.enter_context(tc.psum_pool(name="psum", bufs=1))
+        ctx.enter_context(tc.manual_schedule())
+
+        x_half = [const.tile([P, B // 2], BF16, name="x_half%d" % h) for h in range(2)]
+        bound_rows = const.tile([P, K_PASS], BF16, name="bound_rows")
+        ident = const.tile([P, P], F32, name="ident")
+        planes = [
+            const.tile([P, SC], U8, name="planes%d" % s, align_bytes=64)
+            for s in range(G // PLANES_PER_TILE)
+        ]
+        h_codes = const.tile([P, G * S], U32, name="h_codes", align_bytes=64)
+        h_scales = const.tile([P, G * S], U8, name="h_scales", align_bytes=64)
+        xg = const.tile([P, B], BF16, name="xg")
+        hi = const.tile([P, G, PACK], BF16, name="hi")
+        lo = const.tile([P, G, PACK], BF16, name="lo")
+        cur = const.tile([P, SC], BF16, name="cur")
+        w_last = [
+            const.tile([P, PACK * N_TILE], U8, name="w_last%d" % b, align_bytes=64)
+            for b in range(NB)
+        ]
+
+        nc.vector.memset(bound_rows[:].bitcast(I32), 0)
+        for s in range(len(planes)):
+            nc.vector.memset(planes[s][:].bitcast(I32), 0)
+        make_identity(nc, ident[:])
+
+        nc.sync.dma_start(out=x_half[0][:], in_=x_dram[:, 0 : B // 2])
+        nc.sync.dma_start(
+            out=bound_rows[0:G, :], in_=avail_bundle.rearrange("(g c) -> g c", c=K_PASS)
+        )
+        nc.sync.dma_start(
+            out=bound_rows[G : 2 * G, :], in_=alloc_bundle.rearrange("(g c) -> g c", c=K_PASS)
+        )
+        nc.sync.dma_start(out=x_half[1][:], in_=x_dram[:, B // 2 : B])
+        for s in range(len(planes)):
+            for q in range(4):
+                nc.sync.dma_start(
+                    out=planes[s][32 * q : 32 * q + 16, :].bitcast(I32),
+                    in_=bun_sc_scales[
+                        PLANES_PER_TILE * s : PLANES_PER_TILE * (s + 1), 4 * q : 4 * q + 4, :
+                    ].bitcast(I32),
+                )
+
+        def load_w(g):
+            w = wpool.tile([P, PACK * SC], U8, name="w", tag="w", align_bytes=64)
+            nc.sync.dma_start(
+                out=w[:].bitcast(I32),
+                in_=bun_sc_words[g].rearrange("p n t -> p (n t)").bitcast(I32),
+            )
+            return w
+
+        w_tiles = {}
+        for g in range(W_BUFS):
+            w_tiles[g] = load_w(g)
+        nc.sync.dma_start(out=cur[:], in_=cur_inven)
+
+        def transpose_chunk(c):
+            xt = psum.tile([P, G_CHUNK, 2, S], F32, name="xt%d" % c, tag="bank%d" % c)
+            for gi in range(G_CHUNK):
+                g = G_CHUNK * c + gi
+                h, gl = divmod(g, G // 2)
+                words = x_half[h][:].bitcast(F32)
+                for u in range(2):
+                    nc.tensor.transpose(
+                        xt[:, gi, u, :], words[:, 256 * gl + u : 256 * (gl + 1) : 2], ident[:]
+                    )
+            nc.scalar.copy(
+                out=xg[:]
+                .bitcast(F32)[:, (CHUNK_COLS // 2) * c : (CHUNK_COLS // 2) * (c + 1)]
+                .rearrange("p (g s u) -> p g s u", g=G_CHUNK, u=2),
+                in_=xt[:].rearrange("p g u s -> p g s u"),
+            )
+
+        for c in range(CHUNKS // 2):
+            transpose_chunk(c)
+        bt = psum.tile([P, 2, P], F32, name="bt", tag="bank6")
+        for u in range(2):
+            nc.tensor.transpose(bt[:, u, :], bound_rows[:].bitcast(F32)[:, u : 256 : 2], ident[:])
+        for c in range(CHUNKS // 2, CHUNKS):
+            transpose_chunk(c)
+
+        bt_vals = bt[:].bitcast(BF16).rearrange("p u (r e) -> p r u e", e=2)
+        nc.vector.tensor_scalar(
+            out=hi[:].rearrange("p g (u e) -> p g u e", e=2),
+            in0=bt_vals[:, 0:G, :, :],
+            scalar1=0.0,
+            scalar2=None,
+            op0=ALU.max,
+        )
+        nc.vector.tensor_scalar(
+            out=lo[:].rearrange("p g (u e) -> p g u e", e=2),
+            in0=bt_vals[:, G : 2 * G, :, :],
+            scalar1=-1.0,
+            scalar2=0.0,
+            op0=ALU.mult,
+            op1=ALU.min,
+        )
+
+        shape4 = [P, G_CHUNK, S, PACK]
+        for c in range(CHUNKS):
+            gs = slice(G_CHUNK * c, G_CHUNK * (c + 1))
+            x_flat = xg[:, CHUNK_COLS * c : CHUNK_COLS * (c + 1)]
+            x4 = x_flat.rearrange("p (g s t) -> p g s t", g=G_CHUNK, t=PACK)
+            c_lo = work.tile([P, CHUNK_COLS], BF16, name="c_lo")
+            c_hi = work.tile([P, CHUNK_COLS], BF16, name="c_hi")
+            inside = work.tile([P, CHUNK_COLS], BF16, name="inside")
+            hg = work.tile([P, CHUNK_COLS], BF16, name="hg", align_bytes=64)
+            nc.vector.tensor_tensor(
+                out=c_lo[:].rearrange("p (g s t) -> p g s t", g=G_CHUNK, t=PACK),
+                in0=x4,
+                in1=lo[:, gs, :].unsqueeze(2).to_broadcast(shape4),
+                op=ALU.max,
+            )
+            nc.vector.tensor_tensor(
+                out=c_hi[:].rearrange("p (g s t) -> p g s t", g=G_CHUNK, t=PACK),
+                in0=c_lo[:].rearrange("p (g s t) -> p g s t", g=G_CHUNK, t=PACK),
+                in1=hi[:, gs, :].unsqueeze(2).to_broadcast(shape4),
+                op=ALU.min,
+            )
+            nc.vector.tensor_tensor(out=inside[:], in0=c_hi[:], in1=x_flat, op=ALU.is_equal)
+            nc.vector.scalar_tensor_tensor(
+                out=hg[:], in0=inside[:], scalar=0.01, in1=x_flat, op0=ALU.max, op1=ALU.mult
+            )
+            cols = slice(G_CHUNK * S * c, G_CHUNK * S * (c + 1))
+            nc.vector.quantize_mx(
+                out=h_codes[:, cols].bitcast(FP8X4), scales=h_scales[:, cols], in_=hg[:]
+            )
+
+        acc = [psum.tile([P, N_TILE], F32, name="acc%d" % b, tag="bank%d" % b) for b in range(NB)]
+
+        def mx_pass(g, b, w_cols):
+            s, k = divmod(g, PLANES_PER_TILE)
+            nc.tensor.matmul_mx(
+                out=acc[b][:],
+                lhsT=h_codes[:, S * g : S * (g + 1)].bitcast(FP8X4),
+                lhsT_scale=h_scales[:, S * g : S * (g + 1)],
+                rhs=w_cols.bitcast(FP8X4),
+                rhs_scale=planes[s][4 * k : P, N_TILE * b : N_TILE * (b + 1)],
+                start=(g == 0),
+                stop=(g == G - 1),
+            )
+
+        for g in range(G - 1):
+            for b in range(NB):
+                mx_pass(g, b, w_tiles[g][:, PACK * N_TILE * b : PACK * N_TILE * (b + 1)])
+            nxt = g + W_BUFS
+            if nxt < G - 1:
+                w_tiles[nxt] = load_w(nxt)
+            if nxt == G - 2:
+                for b in range(NB):
+                    nc.sync.dma_start(
+                        out=w_last[b][:].bitcast(I32),
+                        in_=bun_sc_words[G - 1, :, N_TILE * b : N_TILE * (b + 1), :]
+                        .rearrange("p n t -> p (n t)")
+                        .bitcast(I32),
+                    )
+
+        for b in range(NB):
+            mx_pass(G - 1, b, w_last[b][:])
+            o = opool.tile([P, N_TILE], F32, name="o")
+            n_cols = slice(N_TILE * b, N_TILE * (b + 1))
+            nc.vector.tensor_tensor(out=o[:], in0=acc[b][:], in1=cur[:, n_cols], op=ALU.add)
+            nc.sync.dma_start(out=out_rows[:, n_cols], in_=o[:])

@@ -25,6 +25,10 @@ CHUNKS = G // G_CHUNK
 CHUNK_COLS = G_CHUNK * S * PACK
 W_BUFS = 7
 PLANES_PER_TILE = 4
+G_TAIL = 2
+TAIL_BANKS = 2
+TAIL_PIECES = NB // TAIL_BANKS
+TAIL_BYTES = PACK * N_TILE * TAIL_BANKS
 
 FLOPS = 2 * S * B * SC
 
@@ -57,9 +61,9 @@ def tile_optblockv2_w_kernel(
         hi = const.tile([P, G, PACK], BF16, name="hi")
         lo = const.tile([P, G, PACK], BF16, name="lo")
         cur = const.tile([P, SC], BF16, name="cur")
-        w_last = [
-            const.tile([P, PACK * N_TILE], U8, name="w_last%d" % b, align_bytes=64)
-            for b in range(NB)
+        w_tail = [
+            const.tile([P, G_TAIL, TAIL_BYTES], U8, name="w_tail%d" % j, align_bytes=64)
+            for j in range(TAIL_PIECES)
         ]
 
         nc.vector.memset(bound_rows[:].bitcast(I32), 0)
@@ -183,23 +187,31 @@ def tile_optblockv2_w_kernel(
                 stop=(g == G - 1),
             )
 
-        for g in range(G - 1):
+        for g in range(G - G_TAIL):
             for b in range(NB):
                 mx_pass(g, b, w_tiles[g][:, PACK * N_TILE * b : PACK * N_TILE * (b + 1)])
             nxt = g + W_BUFS
-            if nxt < G - 1:
+            if nxt < G - G_TAIL:
                 w_tiles[nxt] = load_w(nxt)
-            if nxt == G - 2:
-                for b in range(NB):
+            if nxt == G - G_TAIL - 1:
+                for j in range(TAIL_PIECES):
                     nc.sync.dma_start(
-                        out=w_last[b][:].bitcast(I32),
-                        in_=bun_sc_words[G - 1, :, N_TILE * b : N_TILE * (b + 1), :]
-                        .rearrange("p n t -> p (n t)")
+                        out=w_tail[j][:].bitcast(I32),
+                        in_=bun_sc_words[
+                            G - G_TAIL : G, :, N_TILE * TAIL_BANKS * j : N_TILE * TAIL_BANKS * (j + 1), :
+                        ]
+                        .rearrange("g p n t -> p g (n t)")
                         .bitcast(I32),
                     )
 
         for b in range(NB):
-            mx_pass(G - 1, b, w_last[b][:])
+            j, bi = divmod(b, TAIL_BANKS)
+            for gi in range(G_TAIL):
+                mx_pass(
+                    G - G_TAIL + gi,
+                    b,
+                    w_tail[j][:, gi, PACK * N_TILE * bi : PACK * N_TILE * (bi + 1)],
+                )
             o = opool.tile([P, N_TILE], F32, name="o")
             n_cols = slice(N_TILE * b, N_TILE * (b + 1))
             nc.vector.tensor_tensor(out=o[:], in0=acc[b][:], in1=cur[:, n_cols], op=ALU.add)

@@ -72,10 +72,10 @@ def tile_optblockv2_w_kernel(
         make_identity(nc, ident[:])
 
         nc.sync.dma_start(out=x_half[0][:], in_=x_dram[:, 0 : B // 2])
-        nc.sync.dma_start(
+        nc.scalar.dma_start(
             out=bound_rows[0:G, :], in_=avail_bundle.rearrange("(g c) -> g c", c=K_PASS)
         )
-        nc.sync.dma_start(
+        nc.scalar.dma_start(
             out=bound_rows[G : 2 * G, :], in_=alloc_bundle.rearrange("(g c) -> g c", c=K_PASS)
         )
         nc.sync.dma_start(out=x_half[1][:], in_=x_dram[:, B // 2 : B])

@@ -23,12 +23,14 @@ NB = SC // N_TILE
 G_CHUNK = 2
 CHUNKS = G // G_CHUNK
 CHUNK_COLS = G_CHUNK * S * PACK
-W_BUFS = 7
+W_PAIR = 2
+PAIR_BUFS = 3
 PLANES_PER_TILE = 4
 G_TAIL = 2
 TAIL_BANKS = 2
 TAIL_PIECES = NB // TAIL_BANKS
 TAIL_BYTES = PACK * N_TILE * TAIL_BANKS
+N_PAIRS = (G - G_TAIL) // W_PAIR
 
 FLOPS = 2 * S * B * SC
 
@@ -42,13 +44,13 @@ def tile_optblockv2_w_kernel(
 
     with ExitStack() as ctx:
         const = ctx.enter_context(tc.tile_pool(name="const", bufs=1))
-        wpool = ctx.enter_context(tc.tile_pool(name="wpool", bufs=W_BUFS))
+        wpool = ctx.enter_context(tc.tile_pool(name="wpool", bufs=PAIR_BUFS))
         work = ctx.enter_context(tc.tile_pool(name="work", bufs=2))
-        opool = ctx.enter_context(tc.tile_pool(name="opool", bufs=NB))
+        opool = ctx.enter_context(tc.tile_pool(name="opool", bufs=TAIL_PIECES))
         psum = ctx.enter_context(tc.psum_pool(name="psum", bufs=1))
         ctx.enter_context(tc.manual_schedule())
 
-        x_half = [const.tile([P, B // 2], BF16, name="x_half%d" % h) for h in range(2)]
+        x_rows = const.tile([P, B], BF16, name="x_rows")
         bound_rows = const.tile([P, K_PASS], BF16, name="bound_rows")
         ident = const.tile([P, P], F32, name="ident")
         planes = [
@@ -71,14 +73,13 @@ def tile_optblockv2_w_kernel(
             nc.vector.memset(planes[s][:].bitcast(I32), 0)
         make_identity(nc, ident[:])
 
-        nc.sync.dma_start(out=x_half[0][:], in_=x_dram[:, 0 : B // 2])
+        nc.sync.dma_start(out=x_rows[:], in_=x_dram)
         nc.scalar.dma_start(
             out=bound_rows[0:G, :], in_=avail_bundle.rearrange("(g c) -> g c", c=K_PASS)
         )
         nc.scalar.dma_start(
             out=bound_rows[G : 2 * G, :], in_=alloc_bundle.rearrange("(g c) -> g c", c=K_PASS)
         )
-        nc.sync.dma_start(out=x_half[1][:], in_=x_dram[:, B // 2 : B])
         for s in range(len(planes)):
             for q in range(4):
                 nc.sync.dma_start(
@@ -88,28 +89,36 @@ def tile_optblockv2_w_kernel(
                     ].bitcast(I32),
                 )
 
-        def load_w(g):
-            w = wpool.tile([P, PACK * SC], U8, name="w", tag="w", align_bytes=64)
-            nc.sync.dma_start(
-                out=w[:].bitcast(I32),
-                in_=bun_sc_words[g].rearrange("p n t -> p (n t)").bitcast(I32),
-            )
+        def load_pair(i):
+            w = wpool.tile([P, W_PAIR, PACK * SC], U8, name="w", tag="w", align_bytes=64)
+            if i < N_PAIRS - 1:
+                nc.sync.dma_start(
+                    out=w[:].bitcast(I32),
+                    in_=bun_sc_words[W_PAIR * i : W_PAIR * (i + 1)]
+                    .rearrange("g p n t -> p g (n t)")
+                    .bitcast(I32),
+                )
+            else:
+                for gi in range(W_PAIR):
+                    nc.sync.dma_start(
+                        out=w[:, gi, :].bitcast(I32),
+                        in_=bun_sc_words[W_PAIR * i + gi].rearrange("p n t -> p (n t)").bitcast(I32),
+                    )
             return w
 
-        w_tiles = {}
-        for g in range(W_BUFS):
-            w_tiles[g] = load_w(g)
+        w_pairs = {}
+        for i in range(PAIR_BUFS):
+            w_pairs[i] = load_pair(i)
         nc.sync.dma_start(out=cur[:], in_=cur_inven)
 
         def transpose_chunk(c):
             xt = psum.tile([P, G_CHUNK, 2, S], F32, name="xt%d" % c, tag="bank%d" % c)
             for gi in range(G_CHUNK):
                 g = G_CHUNK * c + gi
-                h, gl = divmod(g, G // 2)
-                words = x_half[h][:].bitcast(F32)
+                words = x_rows[:].bitcast(F32)
                 for u in range(2):
                     nc.tensor.transpose(
-                        xt[:, gi, u, :], words[:, 256 * gl + u : 256 * (gl + 1) : 2], ident[:]
+                        xt[:, gi, u, :], words[:, 256 * g + u : 256 * (g + 1) : 2], ident[:]
                     )
             nc.scalar.copy(
                 out=xg[:]
@@ -187,13 +196,18 @@ def tile_optblockv2_w_kernel(
                 stop=(g == G - 1),
             )
 
-        for g in range(G - G_TAIL):
-            for b in range(NB):
-                mx_pass(g, b, w_tiles[g][:, PACK * N_TILE * b : PACK * N_TILE * (b + 1)])
-            nxt = g + W_BUFS
-            if nxt < G - G_TAIL:
-                w_tiles[nxt] = load_w(nxt)
-            if nxt == G - G_TAIL - 1:
+        for i in range(N_PAIRS):
+            for gi in range(W_PAIR):
+                for b in range(NB):
+                    mx_pass(
+                        W_PAIR * i + gi,
+                        b,
+                        w_pairs[i][:, gi, PACK * N_TILE * b : PACK * N_TILE * (b + 1)],
+                    )
+            nxt = i + PAIR_BUFS
+            if nxt < N_PAIRS:
+                w_pairs[nxt] = load_pair(nxt)
+            if nxt == N_PAIRS - 1:
                 for j in range(TAIL_PIECES):
                     nc.sync.dma_start(
                         out=w_tail[j][:].bitcast(I32),
@@ -204,15 +218,24 @@ def tile_optblockv2_w_kernel(
                         .bitcast(I32),
                     )
 
-        for b in range(NB):
-            j, bi = divmod(b, TAIL_BANKS)
-            for gi in range(G_TAIL):
-                mx_pass(
-                    G - G_TAIL + gi,
-                    b,
-                    w_tail[j][:, gi, PACK * N_TILE * bi : PACK * N_TILE * (bi + 1)],
+        for j in range(TAIL_PIECES):
+            o = opool.tile([P, TAIL_BANKS * N_TILE], F32, name="o")
+            for bi in range(TAIL_BANKS):
+                b = TAIL_BANKS * j + bi
+                for gi in range(G_TAIL):
+                    mx_pass(
+                        G - G_TAIL + gi,
+                        b,
+                        w_tail[j][:, gi, PACK * N_TILE * bi : PACK * N_TILE * (bi + 1)],
+                    )
+                n_cols = slice(N_TILE * b, N_TILE * (b + 1))
+                o_cols = slice(N_TILE * bi, N_TILE * (bi + 1))
+                nc.vector.tensor_tensor(
+                    out=o[:, o_cols], in0=acc[b][:], in1=cur[:, n_cols], op=ALU.add
                 )
-            o = opool.tile([P, N_TILE], F32, name="o")
-            n_cols = slice(N_TILE * b, N_TILE * (b + 1))
-            nc.vector.tensor_tensor(out=o[:], in0=acc[b][:], in1=cur[:, n_cols], op=ALU.add)
-            nc.sync.dma_start(out=out_rows[:, n_cols], in_=o[:])
+                if j == TAIL_PIECES - 1:
+                    nc.sync.dma_start(out=out_rows[:, n_cols], in_=o[:, o_cols])
+            if j < TAIL_PIECES - 1:
+                nc.sync.dma_start(
+                    out=out_rows[:, TAIL_BANKS * N_TILE * j : TAIL_BANKS * N_TILE * (j + 1)], in_=o[:]
+                )

@@ -81,12 +81,19 @@ def tile_optblockv2_w_kernel(
             out=bound_rows[G : 2 * G, :], in_=alloc_bundle.rearrange("(g c) -> g c", c=K_PASS)
         )
         for s in range(len(planes)):
-            for q in range(4):
+            for q in range(2):
                 nc.sync.dma_start(
                     out=planes[s][32 * q : 32 * q + 16, :].bitcast(I32),
                     in_=bun_sc_scales[
                         PLANES_PER_TILE * s : PLANES_PER_TILE * (s + 1), 4 * q : 4 * q + 4, :
                     ].bitcast(I32),
+                )
+            for q in range(2, 4):
+                nc.scalar.dma_start(
+                    out=planes[s][32 * q : 32 * q + 16, :].bitcast(F32),
+                    in_=bun_sc_scales[
+                        PLANES_PER_TILE * s : PLANES_PER_TILE * (s + 1), 4 * q : 4 * q + 4, :
+                    ].bitcast(F32),
                 )
 
         def load_pair(i):

@@ -31,6 +31,7 @@ TAIL_BANKS = 2
 TAIL_PIECES = NB // TAIL_BANKS
 TAIL_BYTES = PACK * N_TILE * TAIL_BANKS
 N_PAIRS = (G - G_TAIL) // W_PAIR
+CUR_EARLY = SC - TAIL_BANKS * N_TILE
 
 FLOPS = 2 * S * B * SC
 
@@ -116,7 +117,7 @@ def tile_optblockv2_w_kernel(
         w_pairs = {}
         for i in range(PAIR_BUFS):
             w_pairs[i] = load_pair(i)
-        nc.sync.dma_start(out=cur[:], in_=cur_inven)
+        nc.sync.dma_start(out=cur[:, 0:CUR_EARLY], in_=cur_inven[:, 0:CUR_EARLY])
 
         def transpose_chunk(c):
             xt = psum.tile([P, G_CHUNK, 2, S], F32, name="xt%d" % c, tag="bank%d" % c)
@@ -224,6 +225,7 @@ def tile_optblockv2_w_kernel(
                         .rearrange("g p n t -> p g (n t)")
                         .bitcast(I32),
                     )
+                nc.sync.dma_start(out=cur[:, CUR_EARLY:SC], in_=cur_inven[:, CUR_EARLY:SC])
 
         for j in range(TAIL_PIECES):
             o = opool.tile([P, TAIL_BANKS * N_TILE], F32, name="o")

@@ -81,21 +81,15 @@ def tile_optblockv2_w_kernel(
         nc.scalar.dma_start(
             out=bound_rows[G : 2 * G, :], in_=alloc_bundle.rearrange("(g c) -> g c", c=K_PASS)
         )
-        for s in range(len(planes)):
-            for q in range(2):
-                nc.sync.dma_start(
-                    out=planes[s][32 * q : 32 * q + 16, :].bitcast(I32),
-                    in_=bun_sc_scales[
-                        PLANES_PER_TILE * s : PLANES_PER_TILE * (s + 1), 4 * q : 4 * q + 4, :
-                    ].bitcast(I32),
-                )
-            for q in range(2, 4):
-                nc.scalar.dma_start(
-                    out=planes[s][32 * q : 32 * q + 16, :].bitcast(F32),
-                    in_=bun_sc_scales[
-                        PLANES_PER_TILE * s : PLANES_PER_TILE * (s + 1), 4 * q : 4 * q + 4, :
-                    ].bitcast(F32),
-                )
+        for scalar_quad, sync_quad in ((0, 2), (3, 1)):
+            for s in range(len(planes)):
+                for queue, q, view in ((nc.scalar, scalar_quad, F32), (nc.sync, sync_quad, I32)):
+                    queue.dma_start(
+                        out=planes[s][32 * q : 32 * q + 16, :].bitcast(view),
+                        in_=bun_sc_scales[
+                            PLANES_PER_TILE * s : PLANES_PER_TILE * (s + 1), 4 * q : 4 * q + 4, :
+                        ].bitcast(view),
+                    )
 
         def load_pair(i):
             w = wpool.tile([P, W_PAIR, PACK * SC], U8, name="w", tag="w", align_bytes=64)

@@ -27,11 +27,10 @@ W_PAIR = 2
 PAIR_BUFS = 3
 PLANES_PER_TILE = 4
 G_TAIL = 2
-TAIL_BANKS = 2
-TAIL_PIECES = NB // TAIL_BANKS
-TAIL_BYTES = PACK * N_TILE * TAIL_BANKS
+TAIL = ((0, 4), (4, 6), (6, 8))
+STORES = ((0, 2), (2, 4), (4, 6), (6, 7), (7, 8))
 N_PAIRS = (G - G_TAIL) // W_PAIR
-CUR_EARLY = SC - TAIL_BANKS * N_TILE
+CUR_EARLY = SC - 2 * N_TILE
 
 FLOPS = 2 * S * B * SC
 
@@ -47,7 +46,7 @@ def tile_optblockv2_w_kernel(
         const = ctx.enter_context(tc.tile_pool(name="const", bufs=1))
         wpool = ctx.enter_context(tc.tile_pool(name="wpool", bufs=PAIR_BUFS))
         work = ctx.enter_context(tc.tile_pool(name="work", bufs=2))
-        opool = ctx.enter_context(tc.tile_pool(name="opool", bufs=TAIL_PIECES))
+        opool = ctx.enter_context(tc.tile_pool(name="opool", bufs=1))
         psum = ctx.enter_context(tc.psum_pool(name="psum", bufs=1))
         ctx.enter_context(tc.manual_schedule())
 
@@ -65,8 +64,8 @@ def tile_optblockv2_w_kernel(
         lo = const.tile([P, G, PACK], BF16, name="lo")
         cur = const.tile([P, SC], BF16, name="cur")
         w_tail = [
-            const.tile([P, G_TAIL, TAIL_BYTES], U8, name="w_tail%d" % j, align_bytes=64)
-            for j in range(TAIL_PIECES)
+            const.tile([P, G_TAIL, PACK * N_TILE * (b1 - b0)], U8, name="w_tail%d" % b0, align_bytes=64)
+            for b0, b1 in TAIL
         ]
 
         nc.vector.memset(bound_rows[:].bitcast(I32), 0)
@@ -210,35 +209,30 @@ def tile_optblockv2_w_kernel(
             if nxt < N_PAIRS:
                 w_pairs[nxt] = load_pair(nxt)
             if nxt == N_PAIRS - 1:
-                for j in range(TAIL_PIECES):
+                for j, (b0, b1) in enumerate(TAIL):
                     nc.sync.dma_start(
                         out=w_tail[j][:].bitcast(I32),
-                        in_=bun_sc_words[
-                            G - G_TAIL : G, :, N_TILE * TAIL_BANKS * j : N_TILE * TAIL_BANKS * (j + 1), :
-                        ]
+                        in_=bun_sc_words[G - G_TAIL : G, :, N_TILE * b0 : N_TILE * b1, :]
                         .rearrange("g p n t -> p g (n t)")
                         .bitcast(I32),
                     )
                 nc.sync.dma_start(out=cur[:, CUR_EARLY:SC], in_=cur_inven[:, CUR_EARLY:SC])
 
-        for j in range(TAIL_PIECES):
-            o = opool.tile([P, TAIL_BANKS * N_TILE], F32, name="o")
-            for bi in range(TAIL_BANKS):
-                b = TAIL_BANKS * j + bi
-                for gi in range(G_TAIL):
-                    mx_pass(
-                        G - G_TAIL + gi,
-                        b,
-                        w_tail[j][:, gi, PACK * N_TILE * bi : PACK * N_TILE * (bi + 1)],
-                    )
-                n_cols = slice(N_TILE * b, N_TILE * (b + 1))
-                o_cols = slice(N_TILE * bi, N_TILE * (bi + 1))
+        for j, (b0, b1) in enumerate(STORES):
+            o = opool.tile([P, (b1 - b0) * N_TILE], F32, name="o%d" % j)
+            for b in range(b0, b1):
+                for piece, (c0, c1) in enumerate(TAIL):
+                    if c0 <= b < c1:
+                        for gi in range(G_TAIL):
+                            mx_pass(
+                                G - G_TAIL + gi,
+                                b,
+                                w_tail[piece][:, gi, PACK * N_TILE * (b - c0) : PACK * N_TILE * (b - c0 + 1)],
+                            )
                 nc.vector.tensor_tensor(
-                    out=o[:, o_cols], in0=acc[b][:], in1=cur[:, n_cols], op=ALU.add
+                    out=o[:, N_TILE * (b - b0) : N_TILE * (b - b0 + 1)],
+                    in0=acc[b][:],
+                    in1=cur[:, N_TILE * b : N_TILE * (b + 1)],
+                    op=ALU.add,
                 )
-                if j == TAIL_PIECES - 1:
-                    nc.sync.dma_start(out=out_rows[:, n_cols], in_=o[:, o_cols])
-            if j < TAIL_PIECES - 1:
-                nc.sync.dma_start(
-                    out=out_rows[:, TAIL_BANKS * N_TILE * j : TAIL_BANKS * N_TILE * (j + 1)], in_=o[:]
-                )
+            nc.sync.dma_start(out=out_rows[:, N_TILE * b0 : N_TILE * b1], in_=o[:])

from contextlib import ExitStack

import concourse.mybir as mybir
from concourse.masks import make_identity

BF16 = mybir.dt.bfloat16
F32 = mybir.dt.float32
I32 = mybir.dt.int32
U32 = mybir.dt.uint32
U8 = mybir.dt.uint8
FP8X4 = mybir.dt.float8_e4m3fn_x4
ALU = mybir.AluOpType

P = 128
S = 128
B = 6144
SC = 4096
PACK = 4
K_PASS = P * PACK
G = B // K_PASS
N_TILE = 512
NB = SC // N_TILE
G_CHUNK = 2
CHUNKS = G // G_CHUNK
CHUNK_COLS = G_CHUNK * S * PACK
W_PAIR = 2
PAIR_BUFS = 3
PLANES_PER_TILE = 4
G_TAIL = 2
TAIL = ((0, 4), (4, 6), (6, 8))
STORES = ((0, 2), (2, 4), (4, 6), (6, 7), (7, 8))
N_PAIRS = (G - G_TAIL) // W_PAIR
CUR_EARLY = SC - 2 * N_TILE

FLOPS = 2 * S * B * SC


def tile_optblockv2_w_kernel(
    tc, proba, cur_inven, bun_sc_words, bun_sc_scales, avail_bundle, alloc_bundle, out
):
    nc = tc.nc
    x_dram = proba.rearrange("(s b) -> s b", b=B)
    out_rows = out.rearrange("o (s n) -> (o s) n", n=SC)

    with ExitStack() as ctx:
        const = ctx.enter_context(tc.tile_pool(name="const", bufs=1))
        wpool = ctx.enter_context(tc.tile_pool(name="wpool", bufs=PAIR_BUFS))
        work = ctx.enter_context(tc.tile_pool(name="work", bufs=2))
        opool = ctx.enter_context(tc.tile_pool(name="opool", bufs=1))
        psum = ctx.enter_context(tc.psum_pool(name="psum", bufs=1))
        ctx.enter_context(tc.manual_schedule())

        x_rows = const.tile([P, B], BF16, name="x_rows")
        bound_rows = const.tile([P, K_PASS], BF16, name="bound_rows")
        ident = const.tile([P, P], F32, name="ident")
        planes = [
            const.tile([P, SC], U8, name="planes%d" % s, align_bytes=64)
            for s in range(G // PLANES_PER_TILE)
        ]
        h_codes = const.tile([P, G * S], U32, name="h_codes", align_bytes=64)
        h_scales = const.tile([P, G * S], U8, name="h_scales", align_bytes=64)
        xg = const.tile([P, B], BF16, name="xg")
        hi = const.tile([P, G, PACK], BF16, name="hi")
        lo = const.tile([P, G, PACK], BF16, name="lo")
        cur = const.tile([P, SC], BF16, name="cur")
        w_tail = [
            const.tile([P, G_TAIL, PACK * N_TILE * (b1 - b0)], U8, name="w_tail%d" % b0, align_bytes=64)
            for b0, b1 in TAIL
        ]

        nc.vector.memset(bound_rows[:].bitcast(I32), 0)
        for s in range(len(planes)):
            nc.vector.memset(planes[s][:].bitcast(I32), 0)
        make_identity(nc, ident[:])

        nc.sync.dma_start(out=x_rows[:], in_=x_dram)
        nc.scalar.dma_start(
            out=bound_rows[0:G, :], in_=avail_bundle.rearrange("(g c) -> g c", c=K_PASS)
        )
        nc.scalar.dma_start(
            out=bound_rows[G : 2 * G, :], in_=alloc_bundle.rearrange("(g c) -> g c", c=K_PASS)
        )
        for scalar_quad, sync_quad in ((0, 2), (3, 1)):
            for s in range(len(planes)):
                for queue, q, view in ((nc.scalar, scalar_quad, F32), (nc.sync, sync_quad, I32)):
                    queue.dma_start(
                        out=planes[s][32 * q : 32 * q + 16, :].bitcast(view),
                        in_=bun_sc_scales[
                            PLANES_PER_TILE * s : PLANES_PER_TILE * (s + 1), 4 * q : 4 * q + 4, :
                        ].bitcast(view),
                    )

        def load_pair(i):
            w = wpool.tile([P, W_PAIR, PACK * SC], U8, name="w", tag="w", align_bytes=64)
            if i < N_PAIRS - 1:
                nc.sync.dma_start(
                    out=w[:].bitcast(I32),
                    in_=bun_sc_words[W_PAIR * i : W_PAIR * (i + 1)]
                    .rearrange("g p n t -> p g (n t)")
                    .bitcast(I32),
                )
            else:
                for gi in range(W_PAIR):
                    nc.sync.dma_start(
                        out=w[:, gi, :].bitcast(I32),
                        in_=bun_sc_words[W_PAIR * i + gi].rearrange("p n t -> p (n t)").bitcast(I32),
                    )
            return w

        w_pairs = {}
        for i in range(PAIR_BUFS):
            w_pairs[i] = load_pair(i)
        nc.sync.dma_start(out=cur[:, 0:CUR_EARLY], in_=cur_inven[:, 0:CUR_EARLY])

        def transpose_chunk(c):
            xt = psum.tile([P, G_CHUNK, 2, S], F32, name="xt%d" % c, tag="bank%d" % c)
            for gi in range(G_CHUNK):
                g = G_CHUNK * c + gi
                words = x_rows[:].bitcast(F32)
                for u in range(2):
                    nc.tensor.transpose(
                        xt[:, gi, u, :], words[:, 256 * g + u : 256 * (g + 1) : 2], ident[:]
                    )
            nc.scalar.copy(
                out=xg[:]
                .bitcast(F32)[:, (CHUNK_COLS // 2) * c : (CHUNK_COLS // 2) * (c + 1)]
                .rearrange("p (g s u) -> p g s u", g=G_CHUNK, u=2),
                in_=xt[:].rearrange("p g u s -> p g s u"),
            )

        for c in range(CHUNKS // 2):
            transpose_chunk(c)
        bt = psum.tile([P, 2, P], F32, name="bt", tag="bank6")
        for u in range(2):
            nc.tensor.transpose(bt[:, u, :], bound_rows[:].bitcast(F32)[:, u : 256 : 2], ident[:])
        for c in range(CHUNKS // 2, CHUNKS):
            transpose_chunk(c)

        bt_vals = bt[:].bitcast(BF16).rearrange("p u (r e) -> p r u e", e=2)
        nc.vector.tensor_scalar(
            out=hi[:].rearrange("p g (u e) -> p g u e", e=2),
            in0=bt_vals[:, 0:G, :, :],
            scalar1=0.0,
            scalar2=None,
            op0=ALU.max,
        )
        nc.vector.tensor_scalar(
            out=lo[:].rearrange("p g (u e) -> p g u e", e=2),
            in0=bt_vals[:, G : 2 * G, :, :],
            scalar1=-1.0,
            scalar2=0.0,
            op0=ALU.mult,
            op1=ALU.min,
        )

        shape4 = [P, G_CHUNK, S, PACK]
        for c in range(CHUNKS):
            gs = slice(G_CHUNK * c, G_CHUNK * (c + 1))
            x_flat = xg[:, CHUNK_COLS * c : CHUNK_COLS * (c + 1)]
            x4 = x_flat.rearrange("p (g s t) -> p g s t", g=G_CHUNK, t=PACK)
            c_lo = work.tile([P, CHUNK_COLS], BF16, name="c_lo")
            c_hi = work.tile([P, CHUNK_COLS], BF16, name="c_hi")
            inside = work.tile([P, CHUNK_COLS], BF16, name="inside")
            hg = work.tile([P, CHUNK_COLS], BF16, name="hg", align_bytes=64)
            nc.vector.tensor_tensor(
                out=c_lo[:].rearrange("p (g s t) -> p g s t", g=G_CHUNK, t=PACK),
                in0=x4,
                in1=lo[:, gs, :].unsqueeze(2).to_broadcast(shape4),
                op=ALU.max,
            )
            nc.vector.tensor_tensor(
                out=c_hi[:].rearrange("p (g s t) -> p g s t", g=G_CHUNK, t=PACK),
                in0=c_lo[:].rearrange("p (g s t) -> p g s t", g=G_CHUNK, t=PACK),
                in1=hi[:, gs, :].unsqueeze(2).to_broadcast(shape4),
                op=ALU.min,
            )
            nc.vector.tensor_tensor(out=inside[:], in0=c_hi[:], in1=x_flat, op=ALU.is_equal)
            nc.vector.scalar_tensor_tensor(
                out=hg[:], in0=inside[:], scalar=0.01, in1=x_flat, op0=ALU.max, op1=ALU.mult
            )
            cols = slice(G_CHUNK * S * c, G_CHUNK * S * (c + 1))
            nc.vector.quantize_mx(
                out=h_codes[:, cols].bitcast(FP8X4), scales=h_scales[:, cols], in_=hg[:]
            )

        acc = [psum.tile([P, N_TILE], F32, name="acc%d" % b, tag="bank%d" % b) for b in range(NB)]

        def mx_pass(g, b, w_cols):
            s, k = divmod(g, PLANES_PER_TILE)
            nc.tensor.matmul_mx(
                out=acc[b][:],
                lhsT=h_codes[:, S * g : S * (g + 1)].bitcast(FP8X4),
                lhsT_scale=h_scales[:, S * g : S * (g + 1)],
                rhs=w_cols.bitcast(FP8X4),
                rhs_scale=planes[s][4 * k : P, N_TILE * b : N_TILE * (b + 1)],
                start=(g == 0),
                stop=(g == G - 1),
            )

        for i in range(N_PAIRS):
            for gi in range(W_PAIR):
                for b in range(NB):
                    mx_pass(
                        W_PAIR * i + gi,
                        b,
                        w_pairs[i][:, gi, PACK * N_TILE * b : PACK * N_TILE * (b + 1)],
                    )
            nxt = i + PAIR_BUFS
            if nxt < N_PAIRS:
                w_pairs[nxt] = load_pair(nxt)
            if nxt == N_PAIRS - 1:
                for j, (b0, b1) in enumerate(TAIL):
                    nc.sync.dma_start(
                        out=w_tail[j][:].bitcast(I32),
                        in_=bun_sc_words[G - G_TAIL : G, :, N_TILE * b0 : N_TILE * b1, :]
                        .rearrange("g p n t -> p g (n t)")
                        .bitcast(I32),
                    )
                nc.sync.dma_start(out=cur[:, CUR_EARLY:SC], in_=cur_inven[:, CUR_EARLY:SC])

        for j, (b0, b1) in enumerate(STORES):
            o = opool.tile([P, (b1 - b0) * N_TILE], F32, name="o%d" % j)
            for b in range(b0, b1):
                for piece, (c0, c1) in enumerate(TAIL):
                    if c0 <= b < c1:
                        for gi in range(G_TAIL):
                            mx_pass(
                                G - G_TAIL + gi,
                                b,
                                w_tail[piece][:, gi, PACK * N_TILE * (b - c0) : PACK * N_TILE * (b - c0 + 1)],
                            )
                nc.vector.tensor_tensor(
                    out=o[:, N_TILE * (b - b0) : N_TILE * (b - b0 + 1)],
                    in0=acc[b][:],
                    in1=cur[:, N_TILE * b : N_TILE * (b + 1)],
                    op=ALU.add,
                )
            nc.sync.dma_start(out=out_rows[:, N_TILE * b0 : N_TILE * b1], in_=o[:])
